import numpy as np
import ml_dtypes


def mxq(x, axis, fmt="e4m3"):
    dtype, down = {"e4m3": (ml_dtypes.float8_e4m3fn, 7), "e5m2": (ml_dtypes.float8_e5m2, 14)}[fmt]
    v = np.moveaxis(np.asarray(x, np.float32).astype(ml_dtypes.bfloat16).astype(np.float64), axis, -1)
    blocks = v.reshape(v.shape[:-1] + (-1, 32))
    amax = np.abs(blocks).max(-1, keepdims=True)
    byte = np.maximum(np.where(amax > 0, np.frexp(amax)[1] - 1 + 127, 0) - down, 1)
    scale = np.exp2(byte - 127.0)
    codes = (blocks / scale).astype(np.float32).astype(dtype).astype(np.float64)
    return np.moveaxis((codes * scale).reshape(v.shape), -1, axis)


WIDE = False


def mx_kscale(k):
    if not WIDE:
        return np.ones(k)
    levels = np.array([20, -20, 10, -10, 0])
    a = np.random.permutation(np.resize(levels, k // 512 * 4)).reshape(k // 512, 4)
    idx = np.arange(k)
    return np.exp2(a[idx // 512, idx % 128 // 32])


BF16 = ml_dtypes.bfloat16


def bf(x):
    return np.asarray(x, np.float32).astype(BF16)


def f64(x):
    return np.asarray(x).astype(np.float64)


B, I, O, G, P = 8192, 128, 512, 5, 3
NB = G + P
K = I * NB
GMIN, GMAX = -1.0, 1.0


def make_grid():
    bound = GMAX - GMIN
    lo = GMIN - P * bound / G
    hi = GMAX + P * bound / G
    return np.linspace(lo, hi, G + 2 * P + 1)


def spline_bases(x, grid, order):
    xe = x[:, :, None]
    bases = np.where((xe >= grid[:-1]) & (xe < grid[1:]), 1.0, 0.0)
    for k in range(1, order + 1):
        left = (xe - grid[: -(k + 1)]) / (grid[k:-1] - grid[: -(k + 1)])
        right = (grid[k + 1:] - xe) / (grid[k + 1:] - grid[1:-k])
        bases = left * bases[:, :, :-1] + right * bases[:, :, 1:]
    return bases


def spline_slopes(x, grid):
    n2 = spline_bases(x, grid, P - 1)
    return P * (n2[:, :, :-1] / (grid[P:-1] - grid[: -(P + 1)]) - n2[:, :, 1:] / (grid[P + 1:] - grid[1:-P]))


def setup_inputs():
    u = mx_kscale(O)
    x = np.random.uniform(GMIN, GMAX, (B, I))
    w = np.random.standard_normal((I, NB, O)) * 1.6 / np.sqrt(I) / u
    g = np.random.standard_normal((B, O)) * np.exp2(np.random.randint(-12, 1, (B, 1))) * u
    return {"x": bf(x), "spline_kernel": bf(w), "grad_out": bf(g)}


def reference(x, spline_kernel, grad_out):
    grid = make_grid()
    m = mxq(f64(grad_out), 1, "e5m2") @ mxq(f64(spline_kernel).reshape(K, O), 1, "e4m3").T
    d = spline_slopes(f64(x), grid)
    return (d * m.reshape(B, I, NB)).sum(axis=2)

@@ -1,0 +1,206 @@
+from contextlib import ExitStack
+import math
+
+import concourse.bass as bass
+import concourse.mybir as mybir
+import concourse.tile as tile
+from concourse.masks import make_identity
+
+FLOPS = 2 * 8192 * 1024 * 512
+
+F32 = mybir.dt.float32
+BF16 = mybir.dt.bfloat16
+U32 = mybir.dt.uint32
+U8 = mybir.dt.uint8
+E4 = mybir.dt.float8_e4m3fn_x4
+E5 = mybir.dt.float8_e5m2_x4
+ALU = mybir.AluOpType
+ACT = mybir.ActivationFunctionType
+
+P = 128
+NT = 64
+T = 4
+NG = NT // T
+H = 0.4
+GAIN = 1.0 / (2.0 * H)
+ROOT = math.sqrt(GAIN)
+
+
+def knot(j):
+    return -2.2 + H * j
+
+
+def tile_densekan_t_kernel(tc, x, spline_kernel, grad_out, out):
+    nc = tc.nc
+    with ExitStack() as ctx:
+        const = ctx.enter_context(tc.tile_pool(name="const", bufs=1))
+        gin = ctx.enter_context(tc.tile_pool(name="gin", bufs=4))
+        two = ctx.enter_context(tc.tile_pool(name="two", bufs=2))
+        tr = ctx.enter_context(tc.psum_pool(name="tr", bufs=2))
+        mx = ctx.enter_context(tc.psum_pool(name="mx", bufs=3))
+
+        g_view = grad_out.rearrange("(p t) o -> p t o", t=NT)
+        x_view = x.rearrange("(p t) i -> p t i", t=NT)
+        o_view = out.rearrange("(p t) i -> p t i", t=NT)
+
+        ident = const.tile([P, P], F32)
+        make_identity(nc, ident[:])
+
+        w_sb = const.tile([P, 8 * 512], BF16)
+        nc.sync.dma_start(out=w_sb[:], in_=spline_kernel.rearrange("i k o -> i (k o)"))
+        x_sb = const.tile([P, NT * P], BF16)
+
+        def load_x(q):
+            nc.sync.dma_start(
+                out=x_sb[:, q * 16 * P : (q + 1) * 16 * P].rearrange("p (t i) -> p t i", t=16),
+                in_=x_view[:, q * 16 : (q + 1) * 16, :],
+            )
+
+        wg = const.tile([P, 8 * 512], BF16, align_bytes=64)
+        wg32 = wg[:].bitcast(F32).rearrange("p (k i u) -> p k i u", k=8, i=P, u=2)
+        w32 = w_sb[:].bitcast(F32)
+        for kk in range(4):
+            wt = tr.tile([P, 2, 2, P], F32, tag="tp")
+            for a in range(2):
+                for u in range(2):
+                    c0 = (2 * kk + a) * 256 + u * P
+                    nc.tensor.transpose(wt[:, a, u, :], w32[:, c0 : c0 + P], ident[:])
+            nc.vector.tensor_copy(
+                out=wg32[:, 2 * kk : 2 * kk + 2, :, :], in_=wt[:].rearrange("p a u i -> p a i u")
+            )
+
+        def plane(k0, n=1):
+            return wg[:, k0 * 512 : (k0 + n) * 512]
+
+        wm2 = const.tile([P, 4 * 512], BF16, align_bytes=64)
+        nc.vector.tensor_scalar_mul(out=wm2[:], in0=plane(2, 4), scalar1=-2.0)
+        sp = const.tile([P, 3 * 2048], BF16, align_bytes=64)
+
+        def slot(a, q, n=1):
+            return sp[:, a * 2048 + q * 512 : a * 2048 + (q + n) * 512]
+
+        nc.vector.tensor_scalar_mul(out=slot(0, 0), in0=plane(2), scalar1=-1.0)
+        nc.vector.tensor_copy(out=slot(0, 1), in_=plane(7))
+        nc.vector.tensor_scalar_mul(out=slot(0, 2), in0=plane(2), scalar1=2.0)
+        nc.vector.memset(slot(0, 3), 0.0)
+        nc.vector.tensor_scalar_mul(out=slot(1, 0), in0=plane(1), scalar1=2.0)
+        nc.vector.tensor_scalar_mul(out=slot(1, 1), in0=plane(6), scalar1=-2.0)
+        nc.vector.tensor_scalar_mul(out=slot(1, 2), in0=plane(1), scalar1=-2.0)
+        nc.vector.memset(slot(1, 3), 0.0)
+        nc.vector.tensor_scalar_mul(out=slot(2, 0), in0=plane(0), scalar1=-1.0)
+        nc.vector.tensor_copy(out=slot(2, 1), in_=plane(5))
+        nc.vector.memset(slot(2, 2, 2), 0.0)
+
+        cp = const.tile([P, 1024], U32, align_bytes=64)
+        sp_s = const.tile([P, 1024], U8, align_bytes=64)
+        nc.vector.quantize_mx(out=cp[:].bitcast(E4), scales=sp_s[:], in_=wg[:])
+        cm = const.tile([P, 512], U32, align_bytes=64)
+        sm = const.tile([P, 512], U8, align_bytes=64)
+        nc.vector.quantize_mx(out=cm[:].bitcast(E4), scales=sm[:], in_=wm2[:])
+        cs = const.tile([P, 3 * 512], U32, align_bytes=64)
+        ss = const.tile([P, 3 * 512], U8, align_bytes=64)
+        for a in range(3):
+            nc.vector.quantize_mx(
+                out=cs[:, a * 512 : (a + 1) * 512].bitcast(E4),
+                scales=ss[:, a * 512 : (a + 1) * 512],
+                in_=sp[:, a * 2048 : (a + 1) * 2048],
+            )
+
+        bank1 = [(cp, sp_s, 384), (cm, sm, 0), (cp, sp_s, 128)]
+        bank2 = [(cs, ss, 0), (cs, ss, 512), (cs, ss, 1024)]
+
+        for g in range(NG):
+            t0 = g * T
+            gt = gin.tile([P, T * 512], BF16)
+            nc.sync.dma_start(
+                out=gt[:].rearrange("p (t o) -> p t o", t=T), in_=g_view[:, t0 : t0 + T, :]
+            )
+            if g % 4 == 0:
+                load_x(g // 4)
+
+            g32 = gt[:].bitcast(F32)
+            gq = two.tile([P, T * 512], BF16, align_bytes=64)
+            gq32 = gq[:].bitcast(F32).rearrange("p (a b u) -> p a b u", a=T, b=P, u=2)
+            for hh in range(T // 2):
+                tp = tr.tile([P, 2, 2, P], F32, tag="tp")
+                for a in range(2):
+                    for u in range(2):
+                        c0 = (2 * hh + a) * 256 + u * P
+                        nc.tensor.transpose(tp[:, a, u, :], g32[:, c0 : c0 + P], ident[:])
+                nc.scalar.copy(
+                    out=gq32[:, 2 * hh : 2 * hh + 2, :, :], in_=tp[:].rearrange("p a u b -> p a b u")
+                )
+            gc = two.tile([P, T * P], U32, align_bytes=64)
+            gs = two.tile([P, T * P], U8, align_bytes=64)
+            nc.vector.quantize_mx(out=gc[:].bitcast(E5), scales=gs[:], in_=gq[:])
+
+            xs = x_sb[:, t0 * P : (t0 + T) * P]
+            chi = two.tile([P, 5, T * P], F32)
+            for jj in range(5):
+                nc.vector.tensor_scalar(
+                    out=chi[:, jj, :], in0=xs, scalar1=knot(3 + jj), scalar2=knot(4 + jj),
+                    op0=ALU.max, op1=ALU.min,
+                )
+            ap = two.tile([P, T, 4, P], F32)
+            bp = two.tile([P, T, 4, P], F32)
+            w2 = two.tile([P, T, 2, P], F32)
+
+            def rise(dst, jj):
+                nc.scalar.activation(
+                    out=dst, in_=chi[:, jj, :].rearrange("p (t i) -> p t i", t=T), func=ACT.Square,
+                    scale=ROOT / H, bias=-ROOT * knot(3 + jj) / H,
+                )
+
+            def fall(dst, jj):
+                nc.scalar.activation(
+                    out=dst, in_=chi[:, jj, :].rearrange("p (t i) -> p t i", t=T), func=ACT.Square,
+                    scale=-ROOT / H, bias=ROOT * knot(4 + jj) / H,
+                )
+
+            for jj in range(4):
+                rise(ap[:, :, jj, :], jj)
+                fall(bp[:, :, jj, :], jj + 1)
+            fall(w2[:, :, 0, :], 0)
+            rise(w2[:, :, 1, :], 4)
+            yr = two.tile([P, T, 512], F32)
+            nc.gpsimd.tensor_tensor(
+                out=yr[:].rearrange("p t c -> p (t c)"),
+                in0=ap[:].rearrange("p t j i -> p (t j i)"),
+                in1=bp[:].rearrange("p t j i -> p (t j i)"),
+                op=ALU.subtract,
+            )
+
+            p1 = two.tile([P, T, 512], F32)
+            p2 = two.tile([P, T, 256], F32)
+            for t in range(T):
+                lw = gc[:, t * P : (t + 1) * P].bitcast(E5)
+                ls = gs[:, t * P : (t + 1) * P]
+                b1 = mx.tile([P, 512], F32)
+                for n, (c, s, o0) in enumerate(bank1):
+                    nc.tensor.matmul_mx(
+                        out=b1[:], lhsT=lw, lhsT_scale=ls, rhs=c[:, o0 : o0 + 512].bitcast(E4),
+                        rhs_scale=s[:, o0 : o0 + 512], start=(n == 0), stop=(n == 2),
+                    )
+                b2 = mx.tile([P, 512], F32)
+                for n, (c, s, o0) in enumerate(bank2):
+                    nc.tensor.matmul_mx(
+                        out=b2[:], lhsT=lw, lhsT_scale=ls, rhs=c[:, o0 : o0 + 512].bitcast(E4),
+                        rhs_scale=s[:, o0 : o0 + 512], start=(n == 0), stop=(n == 2),
+                    )
+                nc.vector.scalar_tensor_tensor(
+                    out=p1[:, t, :], in0=yr[:, t, :], scalar=GAIN, in1=b1[:], op0=ALU.add, op1=ALU.mult
+                )
+                nc.vector.tensor_tensor(
+                    out=p2[:, t, :], in0=w2[:, t, :, :].rearrange("p j i -> p (j i)"), in1=b2[:, 0:256],
+                    op=ALU.mult,
+                )
+                nc.vector.scalar_tensor_tensor(
+                    out=p2[:, t, 0:P], in0=b2[:, 256:384], scalar=GAIN, in1=p2[:, t, 0:P],
+                    op0=ALU.mult, op1=ALU.add,
+                )
+            s1 = two.tile([P, T, 256], F32)
+            nc.vector.tensor_tensor(out=s1[:], in0=p1[:, :, 0:256], in1=p1[:, :, 256:512], op=ALU.add)
+            nc.vector.tensor_tensor(out=s1[:], in0=s1[:], in1=p2[:], op=ALU.add)
+            ot = two.tile([P, T, P], F32)
+            nc.vector.tensor_tensor(out=ot[:], in0=s1[:, :, 0:P], in1=s1[:, :, P:256], op=ALU.add)
+            nc.sync.dma_start(out=o_view[:, t0 : t0 + T, :], in_=ot[:])

@@ -1,9 +1,7 @@
 from contextlib import ExitStack
 import math
 
-import concourse.bass as bass
 import concourse.mybir as mybir
-import concourse.tile as tile
 from concourse.masks import make_identity
 
 FLOPS = 2 * 8192 * 1024 * 512
@@ -20,7 +18,8 @@ ACT = mybir.ActivationFunctionType
 P = 128
 NT = 64
 T = 4
-NG = NT // T
+CW = T * P
+NC = NT // T
 H = 0.4
 GAIN = 1.0 / (2.0 * H)
 ROOT = math.sqrt(GAIN)
@@ -36,15 +35,15 @@ def tile_densekan_t_kernel(tc, x, spline_kernel, grad_out, out):
         const = ctx.enter_context(tc.tile_pool(name="const", bufs=1))
         gin = ctx.enter_context(tc.tile_pool(name="gin", bufs=4))
         two = ctx.enter_context(tc.tile_pool(name="two", bufs=2))
-        tr = ctx.enter_context(tc.psum_pool(name="tr", bufs=2))
-        mx = ctx.enter_context(tc.psum_pool(name="mx", bufs=3))
+        three = ctx.enter_context(tc.tile_pool(name="three", bufs=3))
+        tr = ctx.enter_context(tc.psum_pool(name="tr", bufs=3))
+        mxp = ctx.enter_context(tc.psum_pool(name="mxp", bufs=4))
+        accp = ctx.enter_context(tc.psum_pool(name="accp", bufs=1))
+        ctx.enter_context(tc.manual_schedule())
 
         g_view = grad_out.rearrange("(p t) o -> p t o", t=NT)
         x_view = x.rearrange("(p t) i -> p t i", t=NT)
         o_view = out.rearrange("(p t) i -> p t i", t=NT)
-
-        ident = const.tile([P, P], F32)
-        make_identity(nc, ident[:])
 
         w_sb = const.tile([P, 8 * 512], BF16)
         nc.sync.dma_start(out=w_sb[:], in_=spline_kernel.rearrange("i k o -> i (k o)"))
@@ -56,6 +55,23 @@ def tile_densekan_t_kernel(tc, x, spline_kernel, grad_out, out):
                 in_=x_view[:, q * 16 : (q + 1) * 16, :],
             )
 
+        live = {}
+
+        def load_g(c):
+            gt = gin.tile([P, T * 512], BF16)
+            nc.sync.dma_start(
+                out=gt[:].rearrange("p (t o) -> p t o", t=T), in_=g_view[:, c * T : (c + 1) * T, :]
+            )
+            live[("gt", c)] = gt
+
+        load_g(0)
+        load_x(0)
+
+        ident = const.tile([P, P], F32)
+        make_identity(nc, ident[:])
+        ident_b = const.tile([P, P], BF16)
+        make_identity(nc, ident_b[:])
+
         wg = const.tile([P, 8 * 512], BF16, align_bytes=64)
         wg32 = wg[:].bitcast(F32).rearrange("p (k i u) -> p k i u", k=8, i=P, u=2)
         w32 = w_sb[:].bitcast(F32)
@@ -65,142 +81,211 @@ def tile_densekan_t_kernel(tc, x, spline_kernel, grad_out, out):
                 for u in range(2):
                     c0 = (2 * kk + a) * 256 + u * P
                     nc.tensor.transpose(wt[:, a, u, :], w32[:, c0 : c0 + P], ident[:])
-            nc.vector.tensor_copy(
-                out=wg32[:, 2 * kk : 2 * kk + 2, :, :], in_=wt[:].rearrange("p a u i -> p a i u")
-            )
-
-        def plane(k0, n=1):
-            return wg[:, k0 * 512 : (k0 + n) * 512]
-
-        wm2 = const.tile([P, 4 * 512], BF16, align_bytes=64)
-        nc.vector.tensor_scalar_mul(out=wm2[:], in0=plane(2, 4), scalar1=-2.0)
-        sp = const.tile([P, 3 * 2048], BF16, align_bytes=64)
-
-        def slot(a, q, n=1):
-            return sp[:, a * 2048 + q * 512 : a * 2048 + (q + n) * 512]
-
-        nc.vector.tensor_scalar_mul(out=slot(0, 0), in0=plane(2), scalar1=-1.0)
-        nc.vector.tensor_copy(out=slot(0, 1), in_=plane(7))
-        nc.vector.tensor_scalar_mul(out=slot(0, 2), in0=plane(2), scalar1=2.0)
-        nc.vector.memset(slot(0, 3), 0.0)
-        nc.vector.tensor_scalar_mul(out=slot(1, 0), in0=plane(1), scalar1=2.0)
-        nc.vector.tensor_scalar_mul(out=slot(1, 1), in0=plane(6), scalar1=-2.0)
-        nc.vector.tensor_scalar_mul(out=slot(1, 2), in0=plane(1), scalar1=-2.0)
-        nc.vector.memset(slot(1, 3), 0.0)
-        nc.vector.tensor_scalar_mul(out=slot(2, 0), in0=plane(0), scalar1=-1.0)
-        nc.vector.tensor_copy(out=slot(2, 1), in_=plane(5))
-        nc.vector.memset(slot(2, 2, 2), 0.0)
-
+            dst = wg32[:, 2 * kk : 2 * kk + 2, :, :]
+            src = wt[:].rearrange("p a u i -> p a i u")
+            if kk % 2 == 0:
+                nc.vector.tensor_copy(out=dst, in_=src)
+            else:
+                nc.scalar.copy(out=dst, in_=src)
         cp = const.tile([P, 1024], U32, align_bytes=64)
-        sp_s = const.tile([P, 1024], U8, align_bytes=64)
-        nc.vector.quantize_mx(out=cp[:].bitcast(E4), scales=sp_s[:], in_=wg[:])
-        cm = const.tile([P, 512], U32, align_bytes=64)
-        sm = const.tile([P, 512], U8, align_bytes=64)
+        sp = const.tile([P, 1024], U8, align_bytes=64)
+        nc.vector.quantize_mx(out=cp[:].bitcast(E4), scales=sp[:], in_=wg[:])
+        wm2 = const.tile([P, 8 * 512], BF16, align_bytes=64)
+        nc.vector.tensor_scalar_mul(out=wm2[:], in0=wg[:], scalar1=-2.0)
+        wp2 = const.tile([P, 512], BF16, align_bytes=64)
+        nc.vector.tensor_scalar_mul(out=wp2[:], in0=wg[:, 2 * 512 : 3 * 512], scalar1=2.0)
+        cm = const.tile([P, 1024], U32, align_bytes=64)
+        sm = const.tile([P, 1024], U8, align_bytes=64)
         nc.vector.quantize_mx(out=cm[:].bitcast(E4), scales=sm[:], in_=wm2[:])
-        cs = const.tile([P, 3 * 512], U32, align_bytes=64)
-        ss = const.tile([P, 3 * 512], U8, align_bytes=64)
-        for a in range(3):
-            nc.vector.quantize_mx(
-                out=cs[:, a * 512 : (a + 1) * 512].bitcast(E4),
-                scales=ss[:, a * 512 : (a + 1) * 512],
-                in_=sp[:, a * 2048 : (a + 1) * 2048],
+        c2 = const.tile([P, P], U32, align_bytes=64)
+        s2 = const.tile([P, P], U8, align_bytes=64)
+        nc.vector.quantize_mx(out=c2[:].bitcast(E4), scales=s2[:], in_=wp2[:])
+
+        def second_difference(j):
+            return [(cp, sp, j), (cm, sm, j - 1), (cp, sp, j - 2)]
+
+        planes = [
+            [(c2, s2, 0), (cm, sm, 1)],
+            second_difference(2),
+            second_difference(7),
+            second_difference(3),
+            second_difference(4),
+            second_difference(5),
+            second_difference(6),
+        ]
+        NP = len(planes)
+
+        def tr_x(c):
+            xp = tr.tile([P, CW], BF16, tag="tp")
+            for a in range(T):
+                t = c * T + a
+                nc.tensor.transpose(xp[:, a * P : (a + 1) * P], x_sb[:, t * P : (t + 1) * P], ident_b[:])
+            live[("xp", c)] = xp
+
+        def ev_x(c):
+            xt = two.tile([P, CW], BF16)
+            nc.scalar.copy(out=xt[:], in_=live[("xp", c)][:])
+            live[("xt", c)] = xt
+
+        def clamps(c):
+            xt = live[("xt", c)]
+            chi = two.tile([P, 5, CW], F32)
+            for jj in range(5):
+                nc.vector.tensor_scalar(
+                    out=chi[:, jj, :], in0=xt[:], scalar1=knot(3 + jj), scalar2=knot(4 + jj),
+                    op0=ALU.max, op1=ALU.min,
+                )
+            live[("chi", c)] = chi
+
+        def squares(c):
+            chi = live[("chi", c)]
+            ap = two.tile([P, 4, CW], F32)
+            bp = two.tile([P, 4, CW], F32)
+            e2 = three.tile([P, 2, CW], F32)
+
+            def rise(dst, jj):
+                nc.scalar.activation(
+                    out=dst, in_=chi[:, jj, :], func=ACT.Square,
+                    scale=ROOT / H, bias=-ROOT * knot(3 + jj) / H,
+                )
+
+            def fall(dst, jj):
+                nc.scalar.activation(
+                    out=dst, in_=chi[:, jj, :], func=ACT.Square,
+                    scale=-ROOT / H, bias=ROOT * knot(4 + jj) / H,
+                )
+
+            fall(e2[:, 0, :], 0)
+            rise(e2[:, 1, :], 4)
+            for jj in range(4):
+                rise(ap[:, jj, :], jj)
+                fall(bp[:, jj, :], jj + 1)
+            live[("ap", c)] = ap
+            live[("bp", c)] = bp
+            live[("e2", c)] = e2
+
+        def combine(c):
+            ap = live[("ap", c)]
+            bp = live[("bp", c)]
+            yr = two.tile([P, 4, CW], F32)
+            nc.vector.tensor_tensor(
+                out=yr[:].rearrange("p j b -> p (j b)"),
+                in0=ap[:].rearrange("p j b -> p (j b)"),
+                in1=bp[:].rearrange("p j b -> p (j b)"),
+                op=ALU.subtract,
             )
+            live[("yr", c)] = yr
 
-        bank1 = [(cp, sp_s, 384), (cm, sm, 0), (cp, sp_s, 128)]
-        bank2 = [(cs, ss, 0), (cs, ss, 512), (cs, ss, 1024)]
-
-        for g in range(NG):
-            t0 = g * T
-            gt = gin.tile([P, T * 512], BF16)
-            nc.sync.dma_start(
-                out=gt[:].rearrange("p (t o) -> p t o", t=T), in_=g_view[:, t0 : t0 + T, :]
-            )
-            if g % 4 == 0:
-                load_x(g // 4)
-
-            g32 = gt[:].bitcast(F32)
-            gq = two.tile([P, T * 512], BF16, align_bytes=64)
-            gq32 = gq[:].bitcast(F32).rearrange("p (a b u) -> p a b u", a=T, b=P, u=2)
+        def tr_g(c):
+            g32 = live[("gt", c)][:].bitcast(F32)
             for hh in range(T // 2):
                 tp = tr.tile([P, 2, 2, P], F32, tag="tp")
                 for a in range(2):
                     for u in range(2):
                         c0 = (2 * hh + a) * 256 + u * P
                         nc.tensor.transpose(tp[:, a, u, :], g32[:, c0 : c0 + P], ident[:])
+                live[("tp", c, hh)] = tp
+
+        def ev_g(c):
+            gq = two.tile([P, T * 512], BF16, align_bytes=64)
+            gq32 = gq[:].bitcast(F32).rearrange("p (a b u) -> p a b u", a=T, b=P, u=2)
+            for hh in range(T // 2):
+                tp = live[("tp", c, hh)]
                 nc.scalar.copy(
                     out=gq32[:, 2 * hh : 2 * hh + 2, :, :], in_=tp[:].rearrange("p a u b -> p a b u")
                 )
-            gc = two.tile([P, T * P], U32, align_bytes=64)
-            gs = two.tile([P, T * P], U8, align_bytes=64)
+            live[("gq", c)] = gq
+
+        def quantise(c):
+            gq = live[("gq", c)]
+            gc = two.tile([P, CW], U32, align_bytes=64)
+            gs = two.tile([P, CW], U8, align_bytes=64)
             nc.vector.quantize_mx(out=gc[:].bitcast(E5), scales=gs[:], in_=gq[:])
+            live[("gc", c)] = (gc, gs)
 
-            xs = x_sb[:, t0 * P : (t0 + T) * P]
-            chi = two.tile([P, 5, T * P], F32)
-            for jj in range(5):
-                nc.vector.tensor_scalar(
-                    out=chi[:, jj, :], in0=xs, scalar1=knot(3 + jj), scalar2=knot(4 + jj),
-                    op0=ALU.max, op1=ALU.min,
+        def mx_plane(c, q):
+            gc, gs = live[("gc", c)]
+            bk = mxp.tile([P, CW], F32)
+            terms = planes[q]
+            for n, (cod, sca, k) in enumerate(terms):
+                nc.tensor.matmul_mx(
+                    out=bk[:], lhsT=cod[:, k * P : (k + 1) * P].bitcast(E4),
+                    lhsT_scale=sca[:, k * P : (k + 1) * P],
+                    rhs=gc[:].bitcast(E5), rhs_scale=gs[:],
+                    start=(n == 0), stop=(n == len(terms) - 1),
                 )
-            ap = two.tile([P, T, 4, P], F32)
-            bp = two.tile([P, T, 4, P], F32)
-            w2 = two.tile([P, T, 2, P], F32)
+            return bk
 
-            def rise(dst, jj):
-                nc.scalar.activation(
-                    out=dst, in_=chi[:, jj, :].rearrange("p (t i) -> p t i", t=T), func=ACT.Square,
-                    scale=ROOT / H, bias=-ROOT * knot(3 + jj) / H,
-                )
-
-            def fall(dst, jj):
-                nc.scalar.activation(
-                    out=dst, in_=chi[:, jj, :].rearrange("p (t i) -> p t i", t=T), func=ACT.Square,
-                    scale=-ROOT / H, bias=ROOT * knot(4 + jj) / H,
-                )
-
-            for jj in range(4):
-                rise(ap[:, :, jj, :], jj)
-                fall(bp[:, :, jj, :], jj + 1)
-            fall(w2[:, :, 0, :], 0)
-            rise(w2[:, :, 1, :], 4)
-            yr = two.tile([P, T, 512], F32)
-            nc.gpsimd.tensor_tensor(
-                out=yr[:].rearrange("p t c -> p (t c)"),
-                in0=ap[:].rearrange("p t j i -> p (t j i)"),
-                in1=bp[:].rearrange("p t j i -> p (t j i)"),
-                op=ALU.subtract,
-            )
-
-            p1 = two.tile([P, T, 512], F32)
-            p2 = two.tile([P, T, 256], F32)
-            for t in range(T):
-                lw = gc[:, t * P : (t + 1) * P].bitcast(E5)
-                ls = gs[:, t * P : (t + 1) * P]
-                b1 = mx.tile([P, 512], F32)
-                for n, (c, s, o0) in enumerate(bank1):
-                    nc.tensor.matmul_mx(
-                        out=b1[:], lhsT=lw, lhsT_scale=ls, rhs=c[:, o0 : o0 + 512].bitcast(E4),
-                        rhs_scale=s[:, o0 : o0 + 512], start=(n == 0), stop=(n == 2),
-                    )
-                b2 = mx.tile([P, 512], F32)
-                for n, (c, s, o0) in enumerate(bank2):
-                    nc.tensor.matmul_mx(
-                        out=b2[:], lhsT=lw, lhsT_scale=ls, rhs=c[:, o0 : o0 + 512].bitcast(E4),
-                        rhs_scale=s[:, o0 : o0 + 512], start=(n == 0), stop=(n == 2),
-                    )
+        def weigh(c, q, bk):
+            pj = live[("pj", c)]
+            if q == 0:
+                nc.scalar.mul(out=pj[:, 0, :], in_=bk[:], mul=GAIN)
+            elif q == 1:
                 nc.vector.scalar_tensor_tensor(
-                    out=p1[:, t, :], in0=yr[:, t, :], scalar=GAIN, in1=b1[:], op0=ALU.add, op1=ALU.mult
+                    out=pj[:, 1, :], in0=live[("e2", c)][:, 0, :], scalar=-1.0, in1=bk[:],
+                    op0=ALU.mult, op1=ALU.mult,
                 )
-                nc.vector.tensor_tensor(
-                    out=p2[:, t, :], in0=w2[:, t, :, :].rearrange("p j i -> p (j i)"), in1=b2[:, 0:256],
-                    op=ALU.mult,
-                )
+            elif q == 2:
+                nc.vector.tensor_tensor(out=pj[:, 2, :], in0=live[("e2", c)][:, 1, :], in1=bk[:], op=ALU.mult)
+            else:
                 nc.vector.scalar_tensor_tensor(
-                    out=p2[:, t, 0:P], in0=b2[:, 256:384], scalar=GAIN, in1=p2[:, t, 0:P],
-                    op0=ALU.mult, op1=ALU.add,
+                    out=pj[:, q, :], in0=live[("yr", c)][:, q - 3, :], scalar=GAIN, in1=bk[:],
+                    op0=ALU.add, op1=ALU.mult,
                 )
-            s1 = two.tile([P, T, 256], F32)
-            nc.vector.tensor_tensor(out=s1[:], in0=p1[:, :, 0:256], in1=p1[:, :, 256:512], op=ALU.add)
-            nc.vector.tensor_tensor(out=s1[:], in0=s1[:], in1=p2[:], op=ALU.add)
-            ot = two.tile([P, T, P], F32)
-            nc.vector.tensor_tensor(out=ot[:], in0=s1[:, :, 0:P], in1=s1[:, :, P:256], op=ALU.add)
-            nc.sync.dma_start(out=o_view[:, t0 : t0 + T, :], in_=ot[:])
+
+        def add_up(c):
+            pj = live[("pj", c)]
+            acc = accp.tile([P, T, P], F32)
+            for a in range(T):
+                for q in range(NP):
+                    nc.tensor.matmul(
+                        out=acc[:, a, :], lhsT=pj[:, q, a * P : (a + 1) * P], rhs=ident[:],
+                        start=(q == 0), stop=(q == NP - 1), is_transpose=True,
+                    )
+            live[("acc", c)] = acc
+
+        def store(c):
+            acc = live[("acc", c)]
+            ot = three.tile([P, T, P], F32)
+            nc.scalar.copy(out=ot[:], in_=acc[:])
+            nc.sync.dma_start(out=o_view[:, c * T : (c + 1) * T, :], in_=ot[:])
+
+        def ok(c):
+            return 0 <= c < NC
+
+        for n in range(-5, NC + 2):
+            if ok(n + 6):
+                load_g(n + 6)
+            if (n + 9) % 4 == 0 and 1 <= (n + 9) // 4 < 4:
+                load_x((n + 9) // 4)
+            if ok(n - 2):
+                store(n - 2)
+            if ok(n + 2):
+                ev_g(n + 2)
+            if ok(n + 4):
+                ev_x(n + 4)
+            if ok(n):
+                pj = two.tile([P, NP, CW], F32)
+                live[("pj", n)] = pj
+                for q in range(3):
+                    weigh(n, q, mx_plane(n, q))
+            if ok(n + 2):
+                squares(n + 2)
+            if ok(n + 3):
+                clamps(n + 3)
+            if ok(n):
+                for q in range(3, 5):
+                    weigh(n, q, mx_plane(n, q))
+            if ok(n + 1):
+                combine(n + 1)
+            if ok(n):
+                for q in range(5, NP):
+                    weigh(n, q, mx_plane(n, q))
+            if ok(n + 1):
+                quantise(n + 1)
+            if ok(n + 3):
+                tr_g(n + 3)
+            if ok(n + 5):
+                tr_x(n + 5)
+            if ok(n - 1):
+                add_up(n - 1)

@@ -105,15 +105,16 @@ def tile_densekan_t_kernel(tc, x, spline_kernel, grad_out, out):
             return [(cp, sp, j), (cm, sm, j - 1), (cp, sp, j - 2)]
 
         planes = [
-            [(c2, s2, 0), (cm, sm, 1)],
             second_difference(2),
             second_difference(7),
+            [(c2, s2, 0), (cm, sm, 1)],
             second_difference(3),
             second_difference(4),
             second_difference(5),
             second_difference(6),
         ]
         NP = len(planes)
+        SUMMED = [0, 3, 5, 6]
 
         def tr_x(c):
             xp = tr.tile([P, CW], BF16, tag="tp")
@@ -219,28 +220,34 @@ def tile_densekan_t_kernel(tc, x, spline_kernel, grad_out, out):
         def weigh(c, q, bk):
             pj = live[("pj", c)]
             if q == 0:
-                nc.scalar.mul(out=pj[:, 0, :], in_=bk[:], mul=GAIN)
-            elif q == 1:
                 nc.vector.scalar_tensor_tensor(
-                    out=pj[:, 1, :], in0=live[("e2", c)][:, 0, :], scalar=-1.0, in1=bk[:],
+                    out=pj[:, 0, :], in0=live[("e2", c)][:, 0, :], scalar=-1.0, in1=bk[:],
                     op0=ALU.mult, op1=ALU.mult,
                 )
+            elif q == 1:
+                nc.vector.tensor_tensor(out=pj[:, 1, :], in0=live[("e2", c)][:, 1, :], in1=bk[:], op=ALU.mult)
             elif q == 2:
-                nc.vector.tensor_tensor(out=pj[:, 2, :], in0=live[("e2", c)][:, 1, :], in1=bk[:], op=ALU.mult)
+                nc.vector.scalar_tensor_tensor(
+                    out=pj[:, 0, :], in0=bk[:], scalar=GAIN, in1=pj[:, 0, :], op0=ALU.mult, op1=ALU.add
+                )
             else:
                 nc.vector.scalar_tensor_tensor(
                     out=pj[:, q, :], in0=live[("yr", c)][:, q - 3, :], scalar=GAIN, in1=bk[:],
                     op0=ALU.add, op1=ALU.mult,
                 )
+                if q == 3:
+                    nc.vector.tensor_tensor(out=pj[:, 0, :], in0=pj[:, 0, :], in1=pj[:, 1, :], op=ALU.add)
+                if q == 5:
+                    nc.vector.tensor_tensor(out=pj[:, 3, :], in0=pj[:, 3, :], in1=pj[:, 4, :], op=ALU.add)
 
         def add_up(c):
             pj = live[("pj", c)]
             acc = accp.tile([P, T, P], F32)
             for a in range(T):
-                for q in range(NP):
+                for q in SUMMED:
                     nc.tensor.matmul(
                         out=acc[:, a, :], lhsT=pj[:, q, a * P : (a + 1) * P], rhs=ident[:],
-                        start=(q == 0), stop=(q == NP - 1), is_transpose=True,
+                        start=(q == SUMMED[0]), stop=(q == SUMMED[-1]), is_transpose=True,
                     )
             live[("acc", c)] = acc
 
@@ -264,25 +271,18 @@ def tile_densekan_t_kernel(tc, x, spline_kernel, grad_out, out):
                 ev_g(n + 2)
             if ok(n + 4):
                 ev_x(n + 4)
-            if ok(n):
-                pj = two.tile([P, NP, CW], F32)
-                live[("pj", n)] = pj
-                for q in range(3):
-                    weigh(n, q, mx_plane(n, q))
             if ok(n + 2):
                 squares(n + 2)
+            if ok(n + 1):
+                quantise(n + 1)
+                combine(n + 1)
             if ok(n + 3):
                 clamps(n + 3)
             if ok(n):
-                for q in range(3, 5):
+                pj = two.tile([P, NP, CW], F32)
+                live[("pj", n)] = pj
+                for q in range(NP):
                     weigh(n, q, mx_plane(n, q))
-            if ok(n + 1):
-                combine(n + 1)
-            if ok(n):
-                for q in range(5, NP):
-                    weigh(n, q, mx_plane(n, q))
-            if ok(n + 1):
-                quantise(n + 1)
             if ok(n + 3):
                 tr_g(n + 3)
             if ok(n + 5):

@@ -46,7 +46,6 @@ def tile_densekan_t_kernel(tc, x, spline_kernel, grad_out, out):
         o_view = out.rearrange("(p t) i -> p t i", t=NT)
 
         w_sb = const.tile([P, 8 * 512], BF16)
-        nc.sync.dma_start(out=w_sb[:], in_=spline_kernel.rearrange("i k o -> i (k o)"))
         x_sb = const.tile([P, NT * P], BF16)
 
         def load_x(q):
@@ -64,8 +63,8 @@ def tile_densekan_t_kernel(tc, x, spline_kernel, grad_out, out):
             )
             live[("gt", c)] = gt
 
-        load_g(0)
         load_x(0)
+        nc.sync.dma_start(out=w_sb[:], in_=spline_kernel.rearrange("i k o -> i (k o)"))
 
         ident = const.tile([P, P], F32)
         make_identity(nc, ident[:])
@@ -73,33 +72,32 @@ def tile_densekan_t_kernel(tc, x, spline_kernel, grad_out, out):
         make_identity(nc, ident_b[:])
 
         wg = const.tile([P, 8 * 512], BF16, align_bytes=64)
-        wg32 = wg[:].bitcast(F32).rearrange("p (k i u) -> p k i u", k=8, i=P, u=2)
-        w32 = w_sb[:].bitcast(F32)
-        for kk in range(4):
-            wt = tr.tile([P, 2, 2, P], F32, tag="tp")
-            for a in range(2):
-                for u in range(2):
-                    c0 = (2 * kk + a) * 256 + u * P
-                    nc.tensor.transpose(wt[:, a, u, :], w32[:, c0 : c0 + P], ident[:])
-            dst = wg32[:, 2 * kk : 2 * kk + 2, :, :]
-            src = wt[:].rearrange("p a u i -> p a i u")
-            if kk % 2 == 0:
-                nc.vector.tensor_copy(out=dst, in_=src)
-            else:
-                nc.scalar.copy(out=dst, in_=src)
+        wm2 = const.tile([P, 8 * 512], BF16, align_bytes=64)
+        wp2 = const.tile([P, 512], BF16, align_bytes=64)
         cp = const.tile([P, 1024], U32, align_bytes=64)
         sp = const.tile([P, 1024], U8, align_bytes=64)
-        nc.vector.quantize_mx(out=cp[:].bitcast(E4), scales=sp[:], in_=wg[:])
-        wm2 = const.tile([P, 8 * 512], BF16, align_bytes=64)
-        nc.vector.tensor_scalar_mul(out=wm2[:], in0=wg[:], scalar1=-2.0)
-        wp2 = const.tile([P, 512], BF16, align_bytes=64)
-        nc.vector.tensor_scalar_mul(out=wp2[:], in0=wg[:, 2 * 512 : 3 * 512], scalar1=2.0)
         cm = const.tile([P, 1024], U32, align_bytes=64)
         sm = const.tile([P, 1024], U8, align_bytes=64)
-        nc.vector.quantize_mx(out=cm[:].bitcast(E4), scales=sm[:], in_=wm2[:])
         c2 = const.tile([P, P], U32, align_bytes=64)
         s2 = const.tile([P, P], U8, align_bytes=64)
-        nc.vector.quantize_mx(out=c2[:].bitcast(E4), scales=s2[:], in_=wp2[:])
+
+        def prepare_w():
+            wg32 = wg[:].bitcast(F32).rearrange("p (k i u) -> p k i u", k=8, i=P, u=2)
+            w32 = w_sb[:].bitcast(F32)
+            for kk in range(4):
+                wt = tr.tile([P, 2, 2, P], F32, tag="tp")
+                for a in range(2):
+                    for u in range(2):
+                        c0 = (2 * kk + a) * 256 + u * P
+                        nc.tensor.transpose(wt[:, a, u, :], w32[:, c0 : c0 + P], ident[:])
+                nc.vector.tensor_copy(
+                    out=wg32[:, 2 * kk : 2 * kk + 2, :, :], in_=wt[:].rearrange("p a u i -> p a i u")
+                )
+            nc.vector.quantize_mx(out=cp[:].bitcast(E4), scales=sp[:], in_=wg[:])
+            nc.vector.tensor_scalar_mul(out=wm2[:], in0=wg[:], scalar1=-2.0)
+            nc.vector.tensor_scalar_mul(out=wp2[:], in0=wg[:, 2 * 512 : 3 * 512], scalar1=2.0)
+            nc.vector.quantize_mx(out=cm[:].bitcast(E4), scales=sm[:], in_=wm2[:])
+            nc.vector.quantize_mx(out=c2[:].bitcast(E4), scales=s2[:], in_=wp2[:])
 
         def second_difference(j):
             return [(cp, sp, j), (cm, sm, j - 1), (cp, sp, j - 2)]
@@ -124,43 +122,53 @@ def tile_densekan_t_kernel(tc, x, spline_kernel, grad_out, out):
             live[("xp", c)] = xp
 
         def ev_x(c):
-            xt = two.tile([P, CW], BF16)
+            xt = three.tile([P, CW], BF16)
             nc.scalar.copy(out=xt[:], in_=live[("xp", c)][:])
             live[("xt", c)] = xt
 
-        def clamps(c):
+        def clamps(c, eng):
             xt = live[("xt", c)]
-            chi = two.tile([P, 5, CW], F32)
-            for jj in range(5):
-                nc.vector.tensor_scalar(
-                    out=chi[:, jj, :], in0=xt[:], scalar1=knot(3 + jj), scalar2=knot(4 + jj),
+            chi = two.tile([P, 3, CW], F32)
+            for jj in range(3):
+                eng.tensor_scalar(
+                    out=chi[:, jj, :], in0=xt[:], scalar1=knot(4 + jj), scalar2=knot(5 + jj),
                     op0=ALU.max, op1=ALU.min,
                 )
             live[("chi", c)] = chi
 
+        def ends(c):
+            xt = live[("xt", c)]
+            rl = two.tile([P, 2, CW], F32)
+            nc.scalar.activation(out=rl[:, 0, :], in_=xt[:], func=ACT.Relu, scale=-1.0 / H, bias=knot(4) / H)
+            nc.scalar.activation(out=rl[:, 1, :], in_=xt[:], func=ACT.Relu, scale=1.0 / H, bias=-knot(7) / H)
+            live[("rl", c)] = rl
+
         def squares(c):
             chi = live[("chi", c)]
+            rl = live[("rl", c)]
             ap = two.tile([P, 4, CW], F32)
             bp = two.tile([P, 4, CW], F32)
             e2 = three.tile([P, 2, CW], F32)
 
-            def rise(dst, jj):
+            def rise(dst, j):
                 nc.scalar.activation(
-                    out=dst, in_=chi[:, jj, :], func=ACT.Square,
-                    scale=ROOT / H, bias=-ROOT * knot(3 + jj) / H,
+                    out=dst, in_=chi[:, j - 4, :], func=ACT.Square,
+                    scale=ROOT / H, bias=-ROOT * knot(j) / H,
                 )
 
-            def fall(dst, jj):
+            def fall(dst, j):
                 nc.scalar.activation(
-                    out=dst, in_=chi[:, jj, :], func=ACT.Square,
-                    scale=-ROOT / H, bias=ROOT * knot(4 + jj) / H,
+                    out=dst, in_=chi[:, j - 4, :], func=ACT.Square,
+                    scale=-ROOT / H, bias=ROOT * knot(j + 1) / H,
                 )
 
-            fall(e2[:, 0, :], 0)
-            rise(e2[:, 1, :], 4)
-            for jj in range(4):
-                rise(ap[:, jj, :], jj)
-                fall(bp[:, jj, :], jj + 1)
+            nc.scalar.activation(out=e2[:, 0, :], in_=rl[:, 0, :], func=ACT.Square, scale=ROOT)
+            nc.scalar.activation(out=e2[:, 1, :], in_=rl[:, 1, :], func=ACT.Square, scale=ROOT)
+            nc.scalar.activation(out=ap[:, 0, :], in_=rl[:, 0, :], func=ACT.Square, scale=-ROOT, bias=ROOT)
+            for j in range(4, 7):
+                fall(bp[:, j - 4, :], j)
+                rise(ap[:, j - 3, :], j)
+            nc.scalar.activation(out=bp[:, 3, :], in_=rl[:, 1, :], func=ACT.Square, scale=-ROOT, bias=ROOT)
             live[("ap", c)] = ap
             live[("bp", c)] = bp
             live[("e2", c)] = e2
@@ -260,32 +268,47 @@ def tile_densekan_t_kernel(tc, x, spline_kernel, grad_out, out):
         def ok(c):
             return 0 <= c < NC
 
+        done = set()
+
+        def run(op, c, *more):
+            if 0 <= c < NC and (op, c) not in done:
+                done.add((op, c))
+                op(c, *more)
+
+        for c in range(3):
+            run(tr_x, c)
+        for c in range(3):
+            run(ev_x, c)
+        run(ends, 0)
+        run(clamps, 0, nc.vector)
+        run(clamps, 1, nc.gpsimd)
+        run(squares, 0)
+        prepare_w()
+
         for n in range(-5, NC + 2):
-            if ok(n + 6):
-                load_g(n + 6)
+            run(load_g, n + 5)
+            run(load_g, n + 6)
             if (n + 9) % 4 == 0 and 1 <= (n + 9) // 4 < 4:
                 load_x((n + 9) // 4)
-            if ok(n - 2):
-                store(n - 2)
-            if ok(n + 2):
-                ev_g(n + 2)
-            if ok(n + 4):
-                ev_x(n + 4)
-            if ok(n + 2):
-                squares(n + 2)
-            if ok(n + 1):
-                quantise(n + 1)
-                combine(n + 1)
-            if ok(n + 3):
-                clamps(n + 3)
+            run(store, n - 2)
+            run(ev_g, n + 2)
+            run(ev_x, n + 4)
+            run(ends, n + 3)
+            run(squares, n + 2)
+            run(quantise, n + 1)
             if ok(n):
                 pj = two.tile([P, NP, CW], F32)
                 live[("pj", n)] = pj
-                for q in range(NP):
+                for q in range(3):
                     weigh(n, q, mx_plane(n, q))
-            if ok(n + 3):
-                tr_g(n + 3)
-            if ok(n + 5):
-                tr_x(n + 5)
-            if ok(n - 1):
-                add_up(n - 1)
+            run(clamps, n + 3, nc.vector)
+            if ok(n):
+                for q in range(3, 5):
+                    weigh(n, q, mx_plane(n, q))
+            run(combine, n + 1)
+            if ok(n):
+                for q in range(5, NP):
+                    weigh(n, q, mx_plane(n, q))
+            run(tr_g, n + 3)
+            run(tr_x, n + 5)
+            run(add_up, n - 1)

@@ -123,52 +123,42 @@ def tile_densekan_t_kernel(tc, x, spline_kernel, grad_out, out):
 
         def ev_x(c):
             xt = three.tile([P, CW], BF16)
-            nc.scalar.copy(out=xt[:], in_=live[("xp", c)][:])
+            nc.vector.tensor_copy(out=xt[:], in_=live[("xp", c)][:])
             live[("xt", c)] = xt
 
         def clamps(c, eng):
             xt = live[("xt", c)]
-            chi = two.tile([P, 3, CW], F32)
-            for jj in range(3):
+            chi = two.tile([P, 5, CW], F32)
+            for jj in range(5):
                 eng.tensor_scalar(
-                    out=chi[:, jj, :], in0=xt[:], scalar1=knot(4 + jj), scalar2=knot(5 + jj),
+                    out=chi[:, jj, :], in0=xt[:], scalar1=knot(3 + jj), scalar2=knot(4 + jj),
                     op0=ALU.max, op1=ALU.min,
                 )
             live[("chi", c)] = chi
 
-        def ends(c):
-            xt = live[("xt", c)]
-            rl = two.tile([P, 2, CW], F32)
-            nc.scalar.activation(out=rl[:, 0, :], in_=xt[:], func=ACT.Relu, scale=-1.0 / H, bias=knot(4) / H)
-            nc.scalar.activation(out=rl[:, 1, :], in_=xt[:], func=ACT.Relu, scale=1.0 / H, bias=-knot(7) / H)
-            live[("rl", c)] = rl
-
         def squares(c):
             chi = live[("chi", c)]
-            rl = live[("rl", c)]
             ap = two.tile([P, 4, CW], F32)
             bp = two.tile([P, 4, CW], F32)
             e2 = three.tile([P, 2, CW], F32)
 
             def rise(dst, j):
                 nc.scalar.activation(
-                    out=dst, in_=chi[:, j - 4, :], func=ACT.Square,
+                    out=dst, in_=chi[:, j - 3, :], func=ACT.Square,
                     scale=ROOT / H, bias=-ROOT * knot(j) / H,
                 )
 
             def fall(dst, j):
                 nc.scalar.activation(
-                    out=dst, in_=chi[:, j - 4, :], func=ACT.Square,
+                    out=dst, in_=chi[:, j - 3, :], func=ACT.Square,
                     scale=-ROOT / H, bias=ROOT * knot(j + 1) / H,
                 )
 
-            nc.scalar.activation(out=e2[:, 0, :], in_=rl[:, 0, :], func=ACT.Square, scale=ROOT)
-            nc.scalar.activation(out=e2[:, 1, :], in_=rl[:, 1, :], func=ACT.Square, scale=ROOT)
-            nc.scalar.activation(out=ap[:, 0, :], in_=rl[:, 0, :], func=ACT.Square, scale=-ROOT, bias=ROOT)
-            for j in range(4, 7):
-                fall(bp[:, j - 4, :], j)
+            fall(e2[:, 0, :], 3)
+            rise(e2[:, 1, :], 7)
+            for j in range(3, 7):
                 rise(ap[:, j - 3, :], j)
-            nc.scalar.activation(out=bp[:, 3, :], in_=rl[:, 1, :], func=ACT.Square, scale=-ROOT, bias=ROOT)
+                fall(bp[:, j - 3, :], j + 1)
             live[("ap", c)] = ap
             live[("bp", c)] = bp
             live[("e2", c)] = e2
@@ -177,12 +167,8 @@ def tile_densekan_t_kernel(tc, x, spline_kernel, grad_out, out):
             ap = live[("ap", c)]
             bp = live[("bp", c)]
             yr = two.tile([P, 4, CW], F32)
-            nc.vector.tensor_tensor(
-                out=yr[:].rearrange("p j b -> p (j b)"),
-                in0=ap[:].rearrange("p j b -> p (j b)"),
-                in1=bp[:].rearrange("p j b -> p (j b)"),
-                op=ALU.subtract,
-            )
+            for jj in range(4):
+                nc.gpsimd.tensor_tensor(out=yr[:, jj, :], in0=ap[:, jj, :], in1=bp[:, jj, :], op=ALU.subtract)
             live[("yr", c)] = yr
 
         def tr_g(c):
@@ -279,9 +265,7 @@ def tile_densekan_t_kernel(tc, x, spline_kernel, grad_out, out):
             run(tr_x, c)
         for c in range(3):
             run(ev_x, c)
-        run(ends, 0)
         run(clamps, 0, nc.vector)
-        run(clamps, 1, nc.gpsimd)
         run(squares, 0)
         prepare_w()
 
@@ -293,7 +277,6 @@ def tile_densekan_t_kernel(tc, x, spline_kernel, grad_out, out):
             run(store, n - 2)
             run(ev_g, n + 2)
             run(ev_x, n + 4)
-            run(ends, n + 3)
             run(squares, n + 2)
             run(quantise, n + 1)
             if ok(n):

@@ -123,7 +123,7 @@ def tile_densekan_t_kernel(tc, x, spline_kernel, grad_out, out):
 
         def ev_x(c):
             xt = three.tile([P, CW], BF16)
-            nc.vector.tensor_copy(out=xt[:], in_=live[("xp", c)][:])
+            nc.scalar.copy(out=xt[:], in_=live[("xp", c)][:])
             live[("xt", c)] = xt
 
         def clamps(c, eng):
@@ -163,13 +163,12 @@ def tile_densekan_t_kernel(tc, x, spline_kernel, grad_out, out):
             live[("bp", c)] = bp
             live[("e2", c)] = e2
 
-        def combine(c):
-            ap = live[("ap", c)]
-            bp = live[("bp", c)]
-            yr = two.tile([P, 4, CW], F32)
-            for jj in range(4):
-                nc.gpsimd.tensor_tensor(out=yr[:, jj, :], in0=ap[:, jj, :], in1=bp[:, jj, :], op=ALU.subtract)
-            live[("yr", c)] = yr
+        yr = const.tile([P, 4, CW], F32)
+
+        def combine(c, jj):
+            nc.gpsimd.tensor_tensor(
+                out=yr[:, jj, :], in0=live[("ap", c)][:, jj, :], in1=live[("bp", c)][:, jj, :], op=ALU.subtract
+            )
 
         def tr_g(c):
             g32 = live[("gt", c)][:].bitcast(F32)
@@ -193,8 +192,8 @@ def tile_densekan_t_kernel(tc, x, spline_kernel, grad_out, out):
 
         def quantise(c):
             gq = live[("gq", c)]
-            gc = two.tile([P, CW], U32, align_bytes=64)
-            gs = two.tile([P, CW], U8, align_bytes=64)
+            gc = three.tile([P, CW], U32, align_bytes=64)
+            gs = three.tile([P, CW], U8, align_bytes=64)
             nc.vector.quantize_mx(out=gc[:].bitcast(E5), scales=gs[:], in_=gq[:])
             live[("gc", c)] = (gc, gs)
 
@@ -226,13 +225,14 @@ def tile_densekan_t_kernel(tc, x, spline_kernel, grad_out, out):
                 )
             else:
                 nc.vector.scalar_tensor_tensor(
-                    out=pj[:, q, :], in0=live[("yr", c)][:, q - 3, :], scalar=GAIN, in1=bk[:],
+                    out=pj[:, q, :], in0=yr[:, q - 3, :], scalar=GAIN, in1=bk[:],
                     op0=ALU.add, op1=ALU.mult,
                 )
-                if q == 3:
-                    nc.vector.tensor_tensor(out=pj[:, 0, :], in0=pj[:, 0, :], in1=pj[:, 1, :], op=ALU.add)
-                if q == 5:
-                    nc.vector.tensor_tensor(out=pj[:, 3, :], in0=pj[:, 3, :], in1=pj[:, 4, :], op=ALU.add)
+
+        def adds(c):
+            pj = live[("pj", c)]
+            nc.vector.tensor_tensor(out=pj[:, 3, :], in0=pj[:, 3, :], in1=pj[:, 4, :], op=ALU.add)
+            nc.vector.tensor_tensor(out=pj[:, 0, :], in0=pj[:, 0, :], in1=pj[:, 1, :], op=ALU.add)
 
         def add_up(c):
             pj = live[("pj", c)]
@@ -269,29 +269,29 @@ def tile_densekan_t_kernel(tc, x, spline_kernel, grad_out, out):
         run(squares, 0)
         prepare_w()
 
-        for n in range(-5, NC + 2):
-            run(load_g, n + 5)
+        for n in range(-7, NC + 2):
             run(load_g, n + 6)
+            run(load_g, n + 7)
             if (n + 9) % 4 == 0 and 1 <= (n + 9) // 4 < 4:
                 load_x((n + 9) // 4)
             run(store, n - 2)
-            run(ev_g, n + 2)
+            run(ev_g, n + 3)
             run(ev_x, n + 4)
             run(squares, n + 2)
-            run(quantise, n + 1)
             if ok(n):
                 pj = two.tile([P, NP, CW], F32)
                 live[("pj", n)] = pj
-                for q in range(3):
+            for q in (3, 4, 5, 6):
+                if ok(n):
                     weigh(n, q, mx_plane(n, q))
+                if ok(n + 1):
+                    combine(n + 1, q - 3)
+            if ok(n):
+                for q in (0, 1, 2):
+                    weigh(n, q, mx_plane(n, q))
+            run(adds, n)
             run(clamps, n + 3, nc.vector)
-            if ok(n):
-                for q in range(3, 5):
-                    weigh(n, q, mx_plane(n, q))
-            run(combine, n + 1)
-            if ok(n):
-                for q in range(5, NP):
-                    weigh(n, q, mx_plane(n, q))
-            run(tr_g, n + 3)
-            run(tr_x, n + 5)
+            run(quantise, n + 2)
+            run(tr_g, n + 4)
             run(add_up, n - 1)
+            run(tr_x, n + 5)

@@ -112,7 +112,7 @@ def tile_densekan_t_kernel(tc, x, spline_kernel, grad_out, out):
             second_difference(6),
         ]
         NP = len(planes)
-        SUMMED = [0, 3, 5, 6]
+        SUMMED = [0, 1, 3, 5, 6]
 
         def tr_x(c):
             xp = tr.tile([P, CW], BF16, tag="tp")
@@ -232,7 +232,6 @@ def tile_densekan_t_kernel(tc, x, spline_kernel, grad_out, out):
         def adds(c):
             pj = live[("pj", c)]
             nc.vector.tensor_tensor(out=pj[:, 3, :], in0=pj[:, 3, :], in1=pj[:, 4, :], op=ALU.add)
-            nc.vector.tensor_tensor(out=pj[:, 0, :], in0=pj[:, 0, :], in1=pj[:, 1, :], op=ALU.add)
 
         def add_up(c):
             pj = live[("pj", c)]

@@ -37,8 +37,7 @@ def tile_densekan_t_kernel(tc, x, spline_kernel, grad_out, out):
         two = ctx.enter_context(tc.tile_pool(name="two", bufs=2))
         three = ctx.enter_context(tc.tile_pool(name="three", bufs=3))
         tr = ctx.enter_context(tc.psum_pool(name="tr", bufs=3))
-        mxp = ctx.enter_context(tc.psum_pool(name="mxp", bufs=4))
-        accp = ctx.enter_context(tc.psum_pool(name="accp", bufs=1))
+        mxp = ctx.enter_context(tc.psum_pool(name="mxp", bufs=5))
         ctx.enter_context(tc.manual_schedule())
 
         g_view = grad_out.rearrange("(p t) o -> p t o", t=NT)
@@ -199,7 +198,7 @@ def tile_densekan_t_kernel(tc, x, spline_kernel, grad_out, out):
 
         def mx_plane(c, q):
             gc, gs = live[("gc", c)]
-            bk = mxp.tile([P, CW], F32)
+            bk = mxp.tile([P, CW], F32, tag="bank")
             terms = planes[q]
             for n, (cod, sca, k) in enumerate(terms):
                 nc.tensor.matmul_mx(
@@ -235,19 +234,22 @@ def tile_densekan_t_kernel(tc, x, spline_kernel, grad_out, out):
 
         def add_up(c):
             pj = live[("pj", c)]
-            acc = accp.tile([P, T, P], F32)
-            for a in range(T):
+            lo = mxp.tile([P, T // 2, P], F32, tag="bank")
+            hi = mxp.tile([P, T // 2, P], F32, tag="bank")
+            for r in range(T // 2):
                 for q in SUMMED:
-                    nc.tensor.matmul(
-                        out=acc[:, a, :], lhsT=pj[:, q, a * P : (a + 1) * P], rhs=ident[:],
-                        start=(q == SUMMED[0]), stop=(q == SUMMED[-1]), is_transpose=True,
-                    )
-            live[("acc", c)] = acc
+                    for bank, a in ((lo, r), (hi, T // 2 + r)):
+                        nc.tensor.matmul(
+                            out=bank[:, r, :], lhsT=pj[:, q, a * P : (a + 1) * P], rhs=ident[:],
+                            start=(q == SUMMED[0]), stop=(q == SUMMED[-1]), is_transpose=True,
+                        )
+            live[("acc", c)] = (lo, hi)
 
         def store(c):
-            acc = live[("acc", c)]
+            lo, hi = live[("acc", c)]
             ot = three.tile([P, T, P], F32)
-            nc.scalar.copy(out=ot[:], in_=acc[:])
+            nc.scalar.copy(out=ot[:, : T // 2, :], in_=lo[:])
+            nc.scalar.copy(out=ot[:, T // 2 :, :], in_=hi[:])
             nc.sync.dma_start(out=o_view[:, c * T : (c + 1) * T, :], in_=ot[:])
 
         def ok(c):

@@ -139,7 +139,6 @@ def tile_densekan_t_kernel(tc, x, spline_kernel, grad_out, out):
             chi = live[("chi", c)]
             ap = two.tile([P, 4, CW], F32)
             bp = two.tile([P, 4, CW], F32)
-            e2 = three.tile([P, 2, CW], F32)
 
             def rise(dst, j):
                 nc.scalar.activation(
@@ -153,13 +152,21 @@ def tile_densekan_t_kernel(tc, x, spline_kernel, grad_out, out):
                     scale=-ROOT / H, bias=ROOT * knot(j + 1) / H,
                 )
 
-            fall(e2[:, 0, :], 3)
-            rise(e2[:, 1, :], 7)
             for j in range(3, 7):
                 rise(ap[:, j - 3, :], j)
                 fall(bp[:, j - 3, :], j + 1)
             live[("ap", c)] = ap
             live[("bp", c)] = bp
+
+        def end_squares(c):
+            chi = live[("chi", c)]
+            e2 = three.tile([P, 2, CW], F32)
+            nc.scalar.activation(
+                out=e2[:, 0, :], in_=chi[:, 0, :], func=ACT.Square, scale=-ROOT / H, bias=ROOT * knot(4) / H
+            )
+            nc.scalar.activation(
+                out=e2[:, 1, :], in_=chi[:, 4, :], func=ACT.Square, scale=ROOT / H, bias=-ROOT * knot(7) / H
+            )
             live[("e2", c)] = e2
 
         yr = const.tile([P, 4, CW], F32)
@@ -278,6 +285,7 @@ def tile_densekan_t_kernel(tc, x, spline_kernel, grad_out, out):
             run(store, n - 2)
             run(ev_g, n + 3)
             run(ev_x, n + 4)
+            run(end_squares, n + 1)
             run(squares, n + 2)
             if ok(n):
                 pj = two.tile([P, NP, CW], F32)
@@ -291,8 +299,8 @@ def tile_densekan_t_kernel(tc, x, spline_kernel, grad_out, out):
                 for q in (0, 1, 2):
                     weigh(n, q, mx_plane(n, q))
             run(adds, n)
-            run(clamps, n + 3, nc.vector)
             run(quantise, n + 2)
+            run(clamps, n + 3, nc.vector)
             run(tr_g, n + 4)
             run(add_up, n - 1)
             run(tr_x, n + 5)

from contextlib import ExitStack
import math

import concourse.mybir as mybir
from concourse.masks import make_identity

FLOPS = 2 * 8192 * 1024 * 512

F32 = mybir.dt.float32
BF16 = mybir.dt.bfloat16
U32 = mybir.dt.uint32
U8 = mybir.dt.uint8
E4 = mybir.dt.float8_e4m3fn_x4
E5 = mybir.dt.float8_e5m2_x4
ALU = mybir.AluOpType
ACT = mybir.ActivationFunctionType

P = 128
NT = 64
T = 4
CW = T * P
NC = NT // T
H = 0.4
GAIN = 1.0 / (2.0 * H)
ROOT = math.sqrt(GAIN)


def knot(j):
    return -2.2 + H * j


def tile_densekan_t_kernel(tc, x, spline_kernel, grad_out, out):
    nc = tc.nc
    with ExitStack() as ctx:
        const = ctx.enter_context(tc.tile_pool(name="const", bufs=1))
        gin = ctx.enter_context(tc.tile_pool(name="gin", bufs=4))
        two = ctx.enter_context(tc.tile_pool(name="two", bufs=2))
        three = ctx.enter_context(tc.tile_pool(name="three", bufs=3))
        tr = ctx.enter_context(tc.psum_pool(name="tr", bufs=3))
        mxp = ctx.enter_context(tc.psum_pool(name="mxp", bufs=5))
        ctx.enter_context(tc.manual_schedule())

        g_view = grad_out.rearrange("(p t) o -> p t o", t=NT)
        x_view = x.rearrange("(p t) i -> p t i", t=NT)
        o_view = out.rearrange("(p t) i -> p t i", t=NT)

        w_sb = const.tile([P, 8 * 512], BF16)
        x_sb = const.tile([P, NT * P], BF16)

        def load_x(q):
            nc.sync.dma_start(
                out=x_sb[:, q * 16 * P : (q + 1) * 16 * P].rearrange("p (t i) -> p t i", t=16),
                in_=x_view[:, q * 16 : (q + 1) * 16, :],
            )

        live = {}

        def load_g(c):
            gt = gin.tile([P, T * 512], BF16)
            nc.sync.dma_start(
                out=gt[:].rearrange("p (t o) -> p t o", t=T), in_=g_view[:, c * T : (c + 1) * T, :]
            )
            live[("gt", c)] = gt

        load_x(0)
        nc.sync.dma_start(out=w_sb[:], in_=spline_kernel.rearrange("i k o -> i (k o)"))

        ident = const.tile([P, P], F32)
        make_identity(nc, ident[:])
        ident_b = const.tile([P, P], BF16)
        make_identity(nc, ident_b[:])

        wg = const.tile([P, 8 * 512], BF16, align_bytes=64)
        wm2 = const.tile([P, 8 * 512], BF16, align_bytes=64)
        wp2 = const.tile([P, 512], BF16, align_bytes=64)
        cp = const.tile([P, 1024], U32, align_bytes=64)
        sp = const.tile([P, 1024], U8, align_bytes=64)
        cm = const.tile([P, 1024], U32, align_bytes=64)
        sm = const.tile([P, 1024], U8, align_bytes=64)
        c2 = const.tile([P, P], U32, align_bytes=64)
        s2 = const.tile([P, P], U8, align_bytes=64)

        def prepare_w():
            wg32 = wg[:].bitcast(F32).rearrange("p (k i u) -> p k i u", k=8, i=P, u=2)
            w32 = w_sb[:].bitcast(F32)
            for kk in range(4):
                wt = tr.tile([P, 2, 2, P], F32, tag="tp")
                for a in range(2):
                    for u in range(2):
                        c0 = (2 * kk + a) * 256 + u * P
                        nc.tensor.transpose(wt[:, a, u, :], w32[:, c0 : c0 + P], ident[:])
                nc.vector.tensor_copy(
                    out=wg32[:, 2 * kk : 2 * kk + 2, :, :], in_=wt[:].rearrange("p a u i -> p a i u")
                )
            nc.vector.quantize_mx(out=cp[:].bitcast(E4), scales=sp[:], in_=wg[:])
            nc.vector.tensor_scalar_mul(out=wm2[:], in0=wg[:], scalar1=-2.0)
            nc.vector.tensor_scalar_mul(out=wp2[:], in0=wg[:, 2 * 512 : 3 * 512], scalar1=2.0)
            nc.vector.quantize_mx(out=cm[:].bitcast(E4), scales=sm[:], in_=wm2[:])
            nc.vector.quantize_mx(out=c2[:].bitcast(E4), scales=s2[:], in_=wp2[:])

        def second_difference(j):
            return [(cp, sp, j), (cm, sm, j - 1), (cp, sp, j - 2)]

        planes = [
            second_difference(2),
            second_difference(7),
            [(c2, s2, 0), (cm, sm, 1)],
            second_difference(3),
            second_difference(4),
            second_difference(5),
            second_difference(6),
        ]
        NP = len(planes)
        SUMMED = [0, 1, 3, 5, 6]

        def tr_x(c):
            xp = tr.tile([P, CW], BF16, tag="tp")
            for a in range(T):
                t = c * T + a
                nc.tensor.transpose(xp[:, a * P : (a + 1) * P], x_sb[:, t * P : (t + 1) * P], ident_b[:])
            live[("xp", c)] = xp

        def ev_x(c):
            xt = three.tile([P, CW], BF16)
            nc.scalar.copy(out=xt[:], in_=live[("xp", c)][:])
            live[("xt", c)] = xt

        def clamps(c, eng):
            xt = live[("xt", c)]
            chi = two.tile([P, 5, CW], F32)
            for jj in range(5):
                eng.tensor_scalar(
                    out=chi[:, jj, :], in0=xt[:], scalar1=knot(3 + jj), scalar2=knot(4 + jj),
                    op0=ALU.max, op1=ALU.min,
                )
            live[("chi", c)] = chi

        def squares(c):
            chi = live[("chi", c)]
            ap = two.tile([P, 4, CW], F32)
            bp = two.tile([P, 4, CW], F32)

            def rise(dst, j):
                nc.scalar.activation(
                    out=dst, in_=chi[:, j - 3, :], func=ACT.Square,
                    scale=ROOT / H, bias=-ROOT * knot(j) / H,
                )

            def fall(dst, j):
                nc.scalar.activation(
                    out=dst, in_=chi[:, j - 3, :], func=ACT.Square,
                    scale=-ROOT / H, bias=ROOT * knot(j + 1) / H,
                )

            for j in range(3, 7):
                rise(ap[:, j - 3, :], j)
                fall(bp[:, j - 3, :], j + 1)
            live[("ap", c)] = ap
            live[("bp", c)] = bp

        def end_squares(c):
            chi = live[("chi", c)]
            e2 = three.tile([P, 2, CW], F32)
            nc.scalar.activation(
                out=e2[:, 0, :], in_=chi[:, 0, :], func=ACT.Square, scale=-ROOT / H, bias=ROOT * knot(4) / H
            )
            nc.scalar.activation(
                out=e2[:, 1, :], in_=chi[:, 4, :], func=ACT.Square, scale=ROOT / H, bias=-ROOT * knot(7) / H
            )
            live[("e2", c)] = e2

        yr = const.tile([P, 4, CW], F32)

        def combine(c, jj):
            nc.gpsimd.tensor_tensor(
                out=yr[:, jj, :], in0=live[("ap", c)][:, jj, :], in1=live[("bp", c)][:, jj, :], op=ALU.subtract
            )

        def tr_g(c):
            g32 = live[("gt", c)][:].bitcast(F32)
            for hh in range(T // 2):
                tp = tr.tile([P, 2, 2, P], F32, tag="tp")
                for a in range(2):
                    for u in range(2):
                        c0 = (2 * hh + a) * 256 + u * P
                        nc.tensor.transpose(tp[:, a, u, :], g32[:, c0 : c0 + P], ident[:])
                live[("tp", c, hh)] = tp

        def ev_g(c):
            gq = two.tile([P, T * 512], BF16, align_bytes=64)
            gq32 = gq[:].bitcast(F32).rearrange("p (a b u) -> p a b u", a=T, b=P, u=2)
            for hh in range(T // 2):
                tp = live[("tp", c, hh)]
                nc.scalar.copy(
                    out=gq32[:, 2 * hh : 2 * hh + 2, :, :], in_=tp[:].rearrange("p a u b -> p a b u")
                )
            live[("gq", c)] = gq

        def quantise(c):
            gq = live[("gq", c)]
            gc = three.tile([P, CW], U32, align_bytes=64)
            gs = three.tile([P, CW], U8, align_bytes=64)
            nc.vector.quantize_mx(out=gc[:].bitcast(E5), scales=gs[:], in_=gq[:])
            live[("gc", c)] = (gc, gs)

        def mx_plane(c, q):
            gc, gs = live[("gc", c)]
            bk = mxp.tile([P, CW], F32, tag="bank")
            terms = planes[q]
            for n, (cod, sca, k) in enumerate(terms):
                nc.tensor.matmul_mx(
                    out=bk[:], lhsT=cod[:, k * P : (k + 1) * P].bitcast(E4),
                    lhsT_scale=sca[:, k * P : (k + 1) * P],
                    rhs=gc[:].bitcast(E5), rhs_scale=gs[:],
                    start=(n == 0), stop=(n == len(terms) - 1),
                )
            return bk

        def weigh(c, q, bk):
            pj = live[("pj", c)]
            if q == 0:
                nc.vector.scalar_tensor_tensor(
                    out=pj[:, 0, :], in0=live[("e2", c)][:, 0, :], scalar=-1.0, in1=bk[:],
                    op0=ALU.mult, op1=ALU.mult,
                )
            elif q == 1:
                nc.vector.tensor_tensor(out=pj[:, 1, :], in0=live[("e2", c)][:, 1, :], in1=bk[:], op=ALU.mult)
            elif q == 2:
                nc.vector.scalar_tensor_tensor(
                    out=pj[:, 0, :], in0=bk[:], scalar=GAIN, in1=pj[:, 0, :], op0=ALU.mult, op1=ALU.add
                )
            else:
                nc.vector.scalar_tensor_tensor(
                    out=pj[:, q, :], in0=yr[:, q - 3, :], scalar=GAIN, in1=bk[:],
                    op0=ALU.add, op1=ALU.mult,
                )

        def adds(c):
            pj = live[("pj", c)]
            nc.vector.tensor_tensor(out=pj[:, 3, :], in0=pj[:, 3, :], in1=pj[:, 4, :], op=ALU.add)

        def add_up(c):
            pj = live[("pj", c)]
            lo = mxp.tile([P, T // 2, P], F32, tag="bank")
            hi = mxp.tile([P, T // 2, P], F32, tag="bank")
            for r in range(T // 2):
                for q in SUMMED:
                    for bank, a in ((lo, r), (hi, T // 2 + r)):
                        nc.tensor.matmul(
                            out=bank[:, r, :], lhsT=pj[:, q, a * P : (a + 1) * P], rhs=ident[:],
                            start=(q == SUMMED[0]), stop=(q == SUMMED[-1]), is_transpose=True,
                        )
            live[("acc", c)] = (lo, hi)

        def store(c):
            lo, hi = live[("acc", c)]
            ot = three.tile([P, T, P], F32)
            nc.scalar.copy(out=ot[:, : T // 2, :], in_=lo[:])
            nc.scalar.copy(out=ot[:, T // 2 :, :], in_=hi[:])
            nc.sync.dma_start(out=o_view[:, c * T : (c + 1) * T, :], in_=ot[:])

        def ok(c):
            return 0 <= c < NC

        done = set()

        def run(op, c, *more):
            if 0 <= c < NC and (op, c) not in done:
                done.add((op, c))
                op(c, *more)

        for c in range(3):
            run(tr_x, c)
        for c in range(3):
            run(ev_x, c)
        run(clamps, 0, nc.vector)
        run(squares, 0)
        prepare_w()

        for n in range(-7, NC + 2):
            run(load_g, n + 6)
            run(load_g, n + 7)
            if (n + 9) % 4 == 0 and 1 <= (n + 9) // 4 < 4:
                load_x((n + 9) // 4)
            run(store, n - 2)
            run(ev_g, n + 3)
            run(ev_x, n + 4)
            run(end_squares, n + 1)
            run(squares, n + 2)
            if ok(n):
                pj = two.tile([P, NP, CW], F32)
                live[("pj", n)] = pj
            for q in (3, 4, 5, 6):
                if ok(n):
                    weigh(n, q, mx_plane(n, q))
                if ok(n + 1):
                    combine(n + 1, q - 3)
            if ok(n):
                for q in (0, 1, 2):
                    weigh(n, q, mx_plane(n, q))
            run(adds, n)
            run(quantise, n + 2)
            run(clamps, n + 3, nc.vector)
            run(tr_g, n + 4)
            run(add_up, n - 1)
            run(tr_x, n + 5)
